import numpy as np
import ml_dtypes


def mxq(x, axis, fmt="e4m3"):
    dtype, down = {"e4m3": (ml_dtypes.float8_e4m3fn, 7), "e5m2": (ml_dtypes.float8_e5m2, 14)}[fmt]
    v = np.moveaxis(np.asarray(x, np.float32).astype(ml_dtypes.bfloat16).astype(np.float64), axis, -1)
    blocks = v.reshape(v.shape[:-1] + (-1, 32))
    amax = np.abs(blocks).max(-1, keepdims=True)
    byte = np.maximum(np.where(amax > 0, np.frexp(amax)[1] - 1 + 127, 0) - down, 1)
    scale = np.exp2(byte - 127.0)
    codes = (blocks / scale).astype(np.float32).astype(dtype).astype(np.float64)
    return np.moveaxis((codes * scale).reshape(v.shape), -1, axis)


WIDE = False


def mx_kscale(k):
    if not WIDE:
        return np.ones(k)
    levels = np.array([20, -20, 10, -10, 0])
    a = np.random.permutation(np.resize(levels, k // 512 * 4)).reshape(k // 512, 4)
    idx = np.arange(k)
    return np.exp2(a[idx // 512, idx % 128 // 32])


BF16 = ml_dtypes.bfloat16


def bf(x):
    return np.asarray(x, np.float32).astype(BF16)


def f64(x):
    return np.asarray(x).astype(np.float64)


N, E, C, D1, D2 = 1024, 2048, 512, 2, 2
T2 = D2 + 1


def shift_down(y, k):
    return np.pad(y, ((k, 0), (0, 0)))[:y.shape[0]] if k > 0 else y


def shift_up(y, k):
    return np.pad(y, ((0, k), (0, 0)))[k:] if k > 0 else y


def log_softmax(z):
    d = z - z.max(-1, keepdims=True)
    return d - np.log(np.exp(d).sum(-1, keepdims=True))


def softmax(z):
    e = np.exp(z - z.max(-1, keepdims=True))
    return e / e.sum(-1, keepdims=True)


def logits(H, W2, b2):
    G = H @ W2
    return sum(shift_down(G[j], D2 - j) for j in range(T2)) + T2 * b2[0]


def setup_inputs():
    s = np.asarray(mx_kscale(N), np.float64)
    t = np.maximum(s, np.maximum(np.concatenate([s[:1], s[:-1]]), np.concatenate([s[:2], s[:-2]])))
    H0 = bf(np.tanh(np.random.standard_normal((N, C))))
    W2 = bf(np.random.standard_normal((T2, C, C)) * 2.0 / np.sqrt(C))
    b2 = bf(np.random.standard_normal((1, C)) * 0.2)
    g = bf(np.random.standard_normal((N, C)) * np.exp2(np.random.randint(-12, 1, (N, 1))) / t[:, None])
    P = softmax(logits(f64(H0), f64(W2), f64(b2)))
    return {"H": bf(f64(H0) * s[:, None]), "W2": W2, "b2": b2, "P": np.asarray(P, np.float32), "grad_out": g}


def reference(H, W2, b2, P, grad_out):
    g = f64(grad_out)
    dZ = g - f64(P) * g.sum(-1, keepdims=True)
    dG = np.stack([shift_up(dZ, D2 - j) for j in range(T2)])
    return mxq(f64(H), 0, "e4m3").T @ mxq(dG, 1, "e5m2")

@@ -1,0 +1,163 @@
+import concourse.mybir as mybir
+from concourse.masks import make_identity
+
+BF16 = mybir.dt.bfloat16
+F32 = mybir.dt.float32
+U32 = mybir.dt.uint32
+U8 = mybir.dt.uint8
+E4M3_X4 = mybir.dt.float8_e4m3fn_x4
+E5M2_X4 = mybir.dt.float8_e5m2_x4
+
+TOKENS = 1024
+CLASSES = 512
+TAPS = 3
+P = 128
+PACK = 4
+K_PASS = P * PACK
+PASSES = TOKENS // K_PASS
+HALO = TAPS - 1
+M_TILES = CLASSES // P
+PSUM_BANKS = 8
+RUN = 4
+
+FLOPS = 2 * TAPS * TOKENS * CLASSES * CLASSES
+BYTES = TOKENS * CLASSES * (2 + 2 + 4) + TAPS * CLASSES * CLASSES * 4
+
+PASS_ORDER = tuple(reversed(range(PASSES)))
+
+
+def rows_of_pass(matrix, c):
+    return matrix[c * K_PASS : (c + 1) * K_PASS, :].rearrange("(p j) w -> p j w", j=PACK)
+
+
+def tile_predictor_pb_v_kernel(tc, h, w2, b2, probs, grad_out, out):
+    nc = tc.nc
+    with (
+        tc.tile_pool(name="keep", bufs=1) as keep,
+        tc.psum_pool(name="psum", bufs=PSUM_BANKS) as psum,
+        tc.manual_schedule(),
+    ):
+
+        def per_pass(shape, dtype, name):
+            return [keep.tile(shape, dtype, name="%s_%d" % (name, c), align_bytes=64) for c in range(PASSES)]
+
+        grad = per_pass([P, PACK, CLASSES], BF16, "grad")
+        prob = per_pass([P, PACK, CLASSES], F32, "prob")
+        hid = per_pass([P, PACK, CLASSES], BF16, "hid")
+        dz = per_pass([P, PACK + HALO, CLASSES], BF16, "dz")
+        neg_sum = per_pass([P, PACK], F32, "neg_sum")
+        negated = per_pass([P, PACK, CLASSES], BF16, "negated")
+        h_grouped = per_pass([P, CLASSES, PACK], BF16, "h_grouped")
+        h_codes = per_pass([P, CLASSES], U32, "h_codes")
+        h_scales = per_pass([P, CLASSES], U8, "h_scales")
+        dg_grouped = [per_pass([P, CLASSES, PACK], BF16, "dg_grouped_%d" % s) for s in range(TAPS)]
+        dg_codes = [per_pass([P, CLASSES], U32, "dg_codes_%d" % s) for s in range(TAPS)]
+        dg_scales = [per_pass([P, CLASSES], U8, "dg_scales_%d" % s) for s in range(TAPS)]
+        result = [keep.tile([P, M_TILES, CLASSES], F32, name="result_%d" % s) for s in range(TAPS)]
+
+        for c in PASS_ORDER:
+            nc.sync.dma_start(out=grad[c][:], in_=rows_of_pass(grad_out, c))
+            for rows in (slice(0, PACK // 2), slice(PACK // 2, PACK)):
+                nc.sync.dma_start(out=prob[c][:, rows, :], in_=rows_of_pass(probs, c)[:, rows, :])
+        for c in PASS_ORDER:
+            nc.sync.dma_start(out=hid[c][:], in_=rows_of_pass(h, c))
+
+        ident = keep.tile([P, P], BF16, name="ident")
+        make_identity(nc, ident[:])
+        from_next = keep.tile([P, P], BF16, name="from_next")
+        nc.gpsimd.memset(from_next[:], 0.0)
+        nc.vector.tensor_copy(out=from_next[:, 0 : P - 1], in_=ident[:, 1:P])
+        from_first = keep.tile([P, P], BF16, name="from_first")
+        nc.gpsimd.memset(from_first[:], 0.0)
+        nc.vector.tensor_copy(out=from_first[:, P - 1 : P], in_=ident[:, 0:1])
+
+        def negative_row_sums(c):
+            for r in range(PACK):
+                nc.scalar.activation(
+                    out=negated[c][:, r, :],
+                    in_=grad[c][:, r, :],
+                    func=mybir.ActivationFunctionType.Copy,
+                    scale=-1.0,
+                    accum_out=neg_sum[c][:, r : r + 1],
+                )
+
+        def make_dz(c):
+            for r in range(PACK):
+                nc.vector.scalar_tensor_tensor(
+                    out=dz[c][:, r, :],
+                    in0=prob[c][:, r, :],
+                    scalar=neg_sum[c][:, r : r + 1],
+                    in1=grad[c][:, r, :],
+                    op0=mybir.AluOpType.mult,
+                    op1=mybir.AluOpType.add,
+                )
+
+        def fetch_halo(c, r):
+            bank = psum.tile([P, CLASSES], F32, tag="bank", name="halo_%d_%d" % (c, r))
+            is_last_pass = c == PASSES - 1
+            nc.tensor.matmul(out=bank[:], lhsT=from_next[:], rhs=dz[c][:, r, :], start=True, stop=is_last_pass)
+            if not is_last_pass:
+                nc.tensor.matmul(out=bank[:], lhsT=from_first[:], rhs=dz[c + 1][:, r, :], start=False, stop=True)
+            nc.scalar.copy(out=dz[c][:, PACK + r, :], in_=bank[:])
+
+        def regroup(copy, rows, grouped):
+            copy(
+                out=grouped[:].rearrange("p (c i) t -> p c t i", i=RUN),
+                in_=rows.rearrange("p t (c i) -> p c t i", i=RUN),
+            )
+
+        def quantise(grouped, packed_dtype, codes, scales):
+            nc.vector.quantize_mx(
+                out=codes[:].bitcast(packed_dtype),
+                scales=scales[:],
+                in_=grouped[:].rearrange("p w t -> p (w t)"),
+            )
+
+        def regroup_and_quantise_dg(s):
+            for c in PASS_ORDER:
+                regroup(nc.vector.tensor_copy, dz[c][:, s : s + PACK, :], dg_grouped[s][c])
+            for c in PASS_ORDER:
+                quantise(dg_grouped[s][c], E5M2_X4, dg_codes[s][c], dg_scales[s][c])
+
+        def multiply_and_store(s, copies):
+            banks = [psum.tile([P, CLASSES], F32, tag="bank", name="acc_%d_%d" % (s, m)) for m in range(M_TILES)]
+            for c in PASS_ORDER:
+                for m in range(M_TILES):
+                    m_cols = slice(m * P, (m + 1) * P)
+                    nc.tensor.matmul_mx(
+                        out=banks[m][:],
+                        lhsT=h_codes[c][:, m_cols].bitcast(E4M3_X4),
+                        lhsT_scale=h_scales[c][:, m_cols],
+                        rhs=dg_codes[s][c][:].bitcast(E5M2_X4),
+                        rhs_scale=dg_scales[s][c][:],
+                        start=(c == PASS_ORDER[0]),
+                        stop=(c == PASS_ORDER[-1]),
+                    )
+            for m in range(M_TILES):
+                copies[m % len(copies)](out=result[s][:, m, :], in_=banks[m][:])
+                nc.sync.dma_start(out=out[TAPS - 1 - s, m * P : (m + 1) * P, :], in_=result[s][:, m, :])
+
+        first_pass, second_pass = PASS_ORDER
+        negative_row_sums(first_pass)
+        make_dz(first_pass)
+        negative_row_sums(second_pass)
+        regroup(nc.vector.tensor_copy, dz[first_pass][:, 0:PACK, :], dg_grouped[0][first_pass])
+        make_dz(second_pass)
+        regroup(nc.vector.tensor_copy, dz[second_pass][:, 0:PACK, :], dg_grouped[0][second_pass])
+        for c in PASS_ORDER:
+            quantise(dg_grouped[0][c], E5M2_X4, dg_codes[0][c], dg_scales[0][c])
+
+        for c in PASS_ORDER:
+            regroup(nc.scalar.copy, hid[c][:], h_grouped[c])
+        for c in PASS_ORDER:
+            quantise(h_grouped[c], E4M3_X4, h_codes[c], h_scales[c])
+
+        for r in range(HALO):
+            for c in PASS_ORDER:
+                fetch_halo(c, r)
+
+        multiply_and_store(0, [nc.scalar.copy])
+        regroup_and_quantise_dg(1)
+        multiply_and_store(1, [nc.scalar.copy])
+        regroup_and_quantise_dg(2)
+        multiply_and_store(2, [nc.scalar.copy, nc.vector.tensor_copy])

@@ -56,8 +56,8 @@ def tile_predictor_pb_v_kernel(tc, h, w2, b2, probs, grad_out, out):
         result = [keep.tile([P, M_TILES, CLASSES], F32, name="result_%d" % s) for s in range(TAPS)]
 
         for c in PASS_ORDER:
-            nc.sync.dma_start(out=grad[c][:], in_=rows_of_pass(grad_out, c))
             for rows in (slice(0, PACK // 2), slice(PACK // 2, PACK)):
+                nc.sync.dma_start(out=grad[c][:, rows, :], in_=rows_of_pass(grad_out, c)[:, rows, :])
                 nc.sync.dma_start(out=prob[c][:, rows, :], in_=rows_of_pass(probs, c)[:, rows, :])
         for c in PASS_ORDER:
             nc.sync.dma_start(out=hid[c][:], in_=rows_of_pass(h, c))
@@ -92,13 +92,14 @@ def tile_predictor_pb_v_kernel(tc, h, w2, b2, probs, grad_out, out):
                     op1=mybir.AluOpType.add,
                 )
 
-        def fetch_halo(c, r):
-            bank = psum.tile([P, CLASSES], F32, tag="bank", name="halo_%d_%d" % (c, r))
+        def fetch_halo(c):
+            bank = psum.tile([P, HALO, CLASSES], BF16, tag="bank", name="halo_%d" % c)
             is_last_pass = c == PASSES - 1
-            nc.tensor.matmul(out=bank[:], lhsT=from_next[:], rhs=dz[c][:, r, :], start=True, stop=is_last_pass)
-            if not is_last_pass:
-                nc.tensor.matmul(out=bank[:], lhsT=from_first[:], rhs=dz[c + 1][:, r, :], start=False, stop=True)
-            nc.scalar.copy(out=dz[c][:, PACK + r, :], in_=bank[:])
+            for r in range(HALO):
+                nc.tensor.matmul(out=bank[:, r, :], lhsT=from_next[:], rhs=dz[c][:, r, :], start=True, stop=is_last_pass)
+                if not is_last_pass:
+                    nc.tensor.matmul(out=bank[:, r, :], lhsT=from_first[:], rhs=dz[c + 1][:, r, :], start=False, stop=True)
+            nc.scalar.copy(out=dz[c][:, PACK : PACK + HALO, :], in_=bank[:])
 
         def regroup(copy, rows, grouped):
             copy(
@@ -113,51 +114,66 @@ def tile_predictor_pb_v_kernel(tc, h, w2, b2, probs, grad_out, out):
                 in_=grouped[:].rearrange("p w t -> p (w t)"),
             )
 
-        def regroup_and_quantise_dg(s):
-            for c in PASS_ORDER:
-                regroup(nc.vector.tensor_copy, dz[c][:, s : s + PACK, :], dg_grouped[s][c])
-            for c in PASS_ORDER:
-                quantise(dg_grouped[s][c], E5M2_X4, dg_codes[s][c], dg_scales[s][c])
+        def regroup_dg(s, c):
+            regroup(nc.vector.tensor_copy, dz[c][:, s : s + PACK, :], dg_grouped[s][c])
 
-        def multiply_and_store(s, copies):
-            banks = [psum.tile([P, CLASSES], F32, tag="bank", name="acc_%d_%d" % (s, m)) for m in range(M_TILES)]
-            for c in PASS_ORDER:
-                for m in range(M_TILES):
-                    m_cols = slice(m * P, (m + 1) * P)
-                    nc.tensor.matmul_mx(
-                        out=banks[m][:],
-                        lhsT=h_codes[c][:, m_cols].bitcast(E4M3_X4),
-                        lhsT_scale=h_scales[c][:, m_cols],
-                        rhs=dg_codes[s][c][:].bitcast(E5M2_X4),
-                        rhs_scale=dg_scales[s][c][:],
-                        start=(c == PASS_ORDER[0]),
-                        stop=(c == PASS_ORDER[-1]),
-                    )
-            for m in range(M_TILES):
-                copies[m % len(copies)](out=result[s][:, m, :], in_=banks[m][:])
-                nc.sync.dma_start(out=out[TAPS - 1 - s, m * P : (m + 1) * P, :], in_=result[s][:, m, :])
+        def quantise_dg(s, c):
+            quantise(dg_grouped[s][c], E5M2_X4, dg_codes[s][c], dg_scales[s][c])
 
-        first_pass, second_pass = PASS_ORDER
-        negative_row_sums(first_pass)
-        make_dz(first_pass)
-        negative_row_sums(second_pass)
-        regroup(nc.vector.tensor_copy, dz[first_pass][:, 0:PACK, :], dg_grouped[0][first_pass])
-        make_dz(second_pass)
-        regroup(nc.vector.tensor_copy, dz[second_pass][:, 0:PACK, :], dg_grouped[0][second_pass])
-        for c in PASS_ORDER:
-            quantise(dg_grouped[0][c], E5M2_X4, dg_codes[0][c], dg_scales[0][c])
-
-        for c in PASS_ORDER:
-            regroup(nc.scalar.copy, hid[c][:], h_grouped[c])
-        for c in PASS_ORDER:
+        def quantise_h(c):
             quantise(h_grouped[c], E4M3_X4, h_codes[c], h_scales[c])
 
-        for r in range(HALO):
-            for c in PASS_ORDER:
-                fetch_halo(c, r)
+        banks = {}
 
-        multiply_and_store(0, [nc.scalar.copy])
-        regroup_and_quantise_dg(1)
-        multiply_and_store(1, [nc.scalar.copy])
-        regroup_and_quantise_dg(2)
-        multiply_and_store(2, [nc.scalar.copy, nc.vector.tensor_copy])
+        def multiply(s, c):
+            if c == PASS_ORDER[0]:
+                banks[s] = [psum.tile([P, CLASSES], F32, tag="bank", name="acc_%d_%d" % (s, m)) for m in range(M_TILES)]
+            for m in range(M_TILES):
+                m_cols = slice(m * P, (m + 1) * P)
+                nc.tensor.matmul_mx(
+                    out=banks[s][m][:],
+                    lhsT=h_codes[c][:, m_cols].bitcast(E4M3_X4),
+                    lhsT_scale=h_scales[c][:, m_cols],
+                    rhs=dg_codes[s][c][:].bitcast(E5M2_X4),
+                    rhs_scale=dg_scales[s][c][:],
+                    start=(c == PASS_ORDER[0]),
+                    stop=(c == PASS_ORDER[-1]),
+                )
+
+        def store(s, copies):
+            for m in range(M_TILES):
+                copies[m % len(copies)](out=result[s][:, m, :], in_=banks[s][m][:])
+                nc.sync.dma_start(out=out[TAPS - 1 - s, m * P : (m + 1) * P, :], in_=result[s][:, m, :])
+
+        a, b = PASS_ORDER
+        negative_row_sums(a)
+        make_dz(a)
+        negative_row_sums(b)
+        regroup_dg(0, a)
+        make_dz(b)
+        regroup(nc.scalar.copy, hid[a][:], h_grouped[a])
+        fetch_halo(a)
+        regroup(nc.scalar.copy, hid[b][:], h_grouped[b])
+        fetch_halo(b)
+        regroup_dg(0, b)
+        quantise_dg(0, a)
+        quantise_dg(0, b)
+        quantise_h(a)
+        multiply(0, a)
+        regroup_dg(1, a)
+        quantise_h(b)
+        multiply(0, b)
+        store(0, [nc.scalar.copy])
+        regroup_dg(1, b)
+        quantise_dg(1, a)
+        multiply(1, a)
+        regroup_dg(2, a)
+        quantise_dg(1, b)
+        multiply(1, b)
+        store(1, [nc.scalar.copy])
+        quantise_dg(2, a)
+        multiply(2, a)
+        regroup_dg(2, b)
+        quantise_dg(2, b)
+        multiply(2, b)
+        store(2, [nc.scalar.copy, nc.vector.tensor_copy])

@@ -148,11 +148,11 @@ def tile_predictor_pb_v_kernel(tc, h, w2, b2, probs, grad_out, out):
         a, b = PASS_ORDER
         negative_row_sums(a)
         make_dz(a)
+        fetch_halo(a)
         negative_row_sums(b)
         regroup_dg(0, a)
         make_dz(b)
         regroup(nc.scalar.copy, hid[a][:], h_grouped[a])
-        fetch_halo(a)
         regroup(nc.scalar.copy, hid[b][:], h_grouped[b])
         fetch_halo(b)
         regroup_dg(0, b)

@@ -1,5 +1,4 @@
 import concourse.mybir as mybir
-from concourse.masks import make_identity
 
 BF16 = mybir.dt.bfloat16
 F32 = mybir.dt.float32
@@ -62,14 +61,7 @@ def tile_predictor_pb_v_kernel(tc, h, w2, b2, probs, grad_out, out):
         for c in PASS_ORDER:
             nc.sync.dma_start(out=hid[c][:], in_=rows_of_pass(h, c))
 
-        ident = keep.tile([P, P], BF16, name="ident")
-        make_identity(nc, ident[:])
-        from_next = keep.tile([P, P], BF16, name="from_next")
-        nc.gpsimd.memset(from_next[:], 0.0)
-        nc.vector.tensor_copy(out=from_next[:, 0 : P - 1], in_=ident[:, 1:P])
-        from_first = keep.tile([P, P], BF16, name="from_first")
-        nc.gpsimd.memset(from_first[:], 0.0)
-        nc.vector.tensor_copy(out=from_first[:, P - 1 : P], in_=ident[:, 0:1])
+        nc.gpsimd.memset(dz[PASSES - 1][:, PACK : PACK + HALO, :], 0.0)
 
         def negative_row_sums(c):
             for r in range(PACK):
@@ -93,13 +85,10 @@ def tile_predictor_pb_v_kernel(tc, h, w2, b2, probs, grad_out, out):
                 )
 
         def fetch_halo(c):
-            bank = psum.tile([P, HALO, CLASSES], BF16, tag="bank", name="halo_%d" % c)
-            is_last_pass = c == PASSES - 1
-            for r in range(HALO):
-                nc.tensor.matmul(out=bank[:, r, :], lhsT=from_next[:], rhs=dz[c][:, r, :], start=True, stop=is_last_pass)
-                if not is_last_pass:
-                    nc.tensor.matmul(out=bank[:, r, :], lhsT=from_first[:], rhs=dz[c + 1][:, r, :], start=False, stop=True)
-            nc.scalar.copy(out=dz[c][:, PACK : PACK + HALO, :], in_=bank[:])
+            for lo, hi in ((0, P // 2), (P // 2, P - 1)):
+                nc.sync.dma_start(out=dz[c][lo:hi, PACK : PACK + HALO, :], in_=dz[c][lo + 1 : hi + 1, 0:HALO, :])
+            if c < PASSES - 1:
+                nc.sync.dma_start(out=dz[c][P - 1 : P, PACK : PACK + HALO, :], in_=dz[c + 1][0:1, 0:HALO, :])
 
         def regroup(copy, rows, grouped):
             copy(

@@ -103,8 +103,8 @@ def tile_predictor_pb_v_kernel(tc, h, w2, b2, probs, grad_out, out):
                 in_=grouped[:].rearrange("p w t -> p (w t)"),
             )
 
-        def regroup_dg(s, c):
-            regroup(nc.vector.tensor_copy, dz[c][:, s : s + PACK, :], dg_grouped[s][c])
+        def regroup_dg(copy, s, c):
+            regroup(copy, dz[c][:, s : s + PACK, :], dg_grouped[s][c])
 
         def quantise_dg(s, c):
             quantise(dg_grouped[s][c], E5M2_X4, dg_codes[s][c], dg_scales[s][c])
@@ -134,35 +134,36 @@ def tile_predictor_pb_v_kernel(tc, h, w2, b2, probs, grad_out, out):
                 copies[m % len(copies)](out=result[s][:, m, :], in_=banks[s][m][:])
                 nc.sync.dma_start(out=out[TAPS - 1 - s, m * P : (m + 1) * P, :], in_=result[s][:, m, :])
 
+        on_vector, on_scalar = nc.vector.tensor_copy, nc.scalar.copy
         a, b = PASS_ORDER
         negative_row_sums(a)
         make_dz(a)
         fetch_halo(a)
         negative_row_sums(b)
-        regroup_dg(0, a)
+        regroup_dg(on_vector, 0, a)
         make_dz(b)
-        regroup(nc.scalar.copy, hid[a][:], h_grouped[a])
-        regroup(nc.scalar.copy, hid[b][:], h_grouped[b])
         fetch_halo(b)
-        regroup_dg(0, b)
+        regroup(on_scalar, hid[a][:], h_grouped[a])
+        regroup(on_scalar, hid[b][:], h_grouped[b])
+        regroup_dg(on_scalar, 1, b)
         quantise_dg(0, a)
-        quantise_dg(0, b)
+        regroup_dg(on_vector, 0, b)
         quantise_h(a)
         multiply(0, a)
-        regroup_dg(1, a)
+        regroup_dg(on_vector, 1, a)
+        quantise_dg(0, b)
         quantise_h(b)
         multiply(0, b)
-        store(0, [nc.scalar.copy])
-        regroup_dg(1, b)
+        store(0, [on_scalar])
         quantise_dg(1, a)
         multiply(1, a)
-        regroup_dg(2, a)
+        regroup_dg(on_vector, 2, a)
         quantise_dg(1, b)
         multiply(1, b)
-        store(1, [nc.scalar.copy])
+        store(1, [on_scalar])
         quantise_dg(2, a)
         multiply(2, a)
-        regroup_dg(2, b)
+        regroup_dg(on_vector, 2, b)
         quantise_dg(2, b)
         multiply(2, b)
-        store(2, [nc.scalar.copy, nc.vector.tensor_copy])
+        store(2, [on_scalar, on_vector])

@@ -54,10 +54,17 @@ def tile_predictor_pb_v_kernel(tc, h, w2, b2, probs, grad_out, out):
         dg_scales = [per_pass([P, CLASSES], U8, "dg_scales_%d" % s) for s in range(TAPS)]
         result = [keep.tile([P, M_TILES, CLASSES], F32, name="result_%d" % s) for s in range(TAPS)]
 
+        def load_rows(tiles, matrix, c, r0, r1):
+            nc.sync.dma_start(out=tiles[c][:, r0:r1, :], in_=rows_of_pass(matrix, c)[:, r0:r1, :])
+
         for c in PASS_ORDER:
-            for rows in (slice(0, PACK // 2), slice(PACK // 2, PACK)):
-                nc.sync.dma_start(out=grad[c][:, rows, :], in_=rows_of_pass(grad_out, c)[:, rows, :])
-                nc.sync.dma_start(out=prob[c][:, rows, :], in_=rows_of_pass(probs, c)[:, rows, :])
+            for r0 in range(0, PACK, 2):
+                load_rows(grad, grad_out, c, r0, r0 + 2)
+                if c == PASS_ORDER[0]:
+                    load_rows(prob, probs, c, r0, r0 + 1)
+                    load_rows(prob, probs, c, r0 + 1, r0 + 2)
+                else:
+                    load_rows(prob, probs, c, r0, r0 + 2)
         for c in PASS_ORDER:
             nc.sync.dma_start(out=hid[c][:], in_=rows_of_pass(h, c))
 

@@ -57,16 +57,16 @@ def tile_predictor_pb_v_kernel(tc, h, w2, b2, probs, grad_out, out):
         def load_rows(tiles, matrix, c, r0, r1):
             nc.sync.dma_start(out=tiles[c][:, r0:r1, :], in_=rows_of_pass(matrix, c)[:, r0:r1, :])
 
-        for c in PASS_ORDER:
-            for r0 in range(0, PACK, 2):
-                load_rows(grad, grad_out, c, r0, r0 + 2)
-                if c == PASS_ORDER[0]:
-                    load_rows(prob, probs, c, r0, r0 + 1)
-                    load_rows(prob, probs, c, r0 + 1, r0 + 2)
-                else:
-                    load_rows(prob, probs, c, r0, r0 + 2)
-        for c in PASS_ORDER:
-            nc.sync.dma_start(out=hid[c][:], in_=rows_of_pass(h, c))
+        first, second = PASS_ORDER
+        for r0 in range(0, PACK, 2):
+            load_rows(grad, grad_out, first, r0, r0 + 2)
+            load_rows(prob, probs, first, r0, r0 + 1)
+            load_rows(prob, probs, first, r0 + 1, r0 + 2)
+        load_rows(grad, grad_out, second, 0, PACK)
+        nc.sync.dma_start(out=hid[first][:], in_=rows_of_pass(h, first))
+        for r0 in range(0, PACK, 2):
+            load_rows(prob, probs, second, r0, r0 + 2)
+        nc.sync.dma_start(out=hid[second][:], in_=rows_of_pass(h, second))
 
         nc.gpsimd.memset(dz[PASSES - 1][:, PACK : PACK + HALO, :], 0.0)
 
@@ -148,12 +148,12 @@ def tile_predictor_pb_v_kernel(tc, h, w2, b2, probs, grad_out, out):
         fetch_halo(a)
         negative_row_sums(b)
         regroup_dg(on_vector, 0, a)
+        quantise_dg(0, a)
         make_dz(b)
         fetch_halo(b)
         regroup(on_scalar, hid[a][:], h_grouped[a])
         regroup(on_scalar, hid[b][:], h_grouped[b])
         regroup_dg(on_scalar, 1, b)
-        quantise_dg(0, a)
         regroup_dg(on_vector, 0, b)
         quantise_h(a)
         multiply(0, a)

@@ -167,10 +167,10 @@ def tile_predictor_pb_v_kernel(tc, h, w2, b2, probs, grad_out, out):
         regroup_dg(on_vector, 2, a)
         quantise_dg(1, b)
         multiply(1, b)
-        store(1, [on_scalar])
         quantise_dg(2, a)
         multiply(2, a)
         regroup_dg(on_vector, 2, b)
         quantise_dg(2, b)
         multiply(2, b)
+        store(1, [on_scalar, on_scalar, on_scalar, on_vector])
         store(2, [on_scalar, on_vector])

@@ -113,6 +113,21 @@ def tile_predictor_pb_v_kernel(tc, h, w2, b2, probs, grad_out, out):
         def regroup_dg(copy, s, c):
             regroup(copy, dz[c][:, s : s + PACK, :], dg_grouped[s][c])
 
+        def regroup_dg_half(s, c, w0):
+            cols = slice(w0, w0 + CLASSES // 2)
+            nc.vector.tensor_copy(
+                out=dg_grouped[s][c][:, cols, :].rearrange("p (c i) t -> p c t i", i=RUN),
+                in_=dz[c][:, s : s + PACK, cols].rearrange("p t (c i) -> p c t i", i=RUN),
+            )
+
+        def quantise_dg_half(s, c, w0):
+            cols = slice(w0, w0 + CLASSES // 2)
+            nc.vector.quantize_mx(
+                out=dg_codes[s][c][:, cols].bitcast(E5M2_X4),
+                scales=dg_scales[s][c][:, cols],
+                in_=dg_grouped[s][c][:, cols, :].rearrange("p w t -> p (w t)"),
+            )
+
         def quantise_dg(s, c):
             quantise(dg_grouped[s][c], E5M2_X4, dg_codes[s][c], dg_scales[s][c])
 
@@ -169,8 +184,10 @@ def tile_predictor_pb_v_kernel(tc, h, w2, b2, probs, grad_out, out):
         multiply(1, b)
         quantise_dg(2, a)
         multiply(2, a)
-        regroup_dg(on_vector, 2, b)
-        quantise_dg(2, b)
+        regroup_dg_half(2, b, 0)
+        regroup_dg_half(2, b, CLASSES // 2)
+        quantise_dg_half(2, b, 0)
+        quantise_dg_half(2, b, CLASSES // 2)
         multiply(2, b)
         store(1, [on_scalar, on_scalar, on_scalar, on_vector])
         store(2, [on_scalar, on_vector])

@@ -1,4 +1,5 @@
 import concourse.mybir as mybir
+from concourse.masks import make_identity
 
 BF16 = mybir.dt.bfloat16
 F32 = mybir.dt.float32
@@ -14,26 +15,31 @@ P = 128
 PACK = 4
 K_PASS = P * PACK
 PASSES = TOKENS // K_PASS
-HALO = TAPS - 1
+EDGE = TAPS - 1
+CHUNK = 16
+CHUNKS = CLASSES // CHUNK
 M_TILES = CLASSES // P
-PSUM_BANKS = 8
 RUN = 4
+SPREAD = 112
 
 FLOPS = 2 * TAPS * TOKENS * CLASSES * CLASSES
 BYTES = TOKENS * CLASSES * (2 + 2 + 4) + TAPS * CLASSES * CLASSES * 4
 
-PASS_ORDER = tuple(reversed(range(PASSES)))
-
 
 def rows_of_pass(matrix, c):
-    return matrix[c * K_PASS : (c + 1) * K_PASS, :].rearrange("(p j) w -> p j w", j=PACK)
+    return matrix[c * K_PASS : (c + 1) * K_PASS, :].rearrange("(t p) w -> p t w", p=P)
+
+
+def edge_rows(matrix, j0, j1):
+    rows = matrix[j0 * P : j1 * P, :].rearrange("(t p) w -> t p w", p=P)[:, 0:EDGE, :]
+    return rows.rearrange("t e (q i) -> (e q) t i", i=CHUNK)
 
 
 def tile_predictor_pb_v_kernel(tc, h, w2, b2, probs, grad_out, out):
     nc = tc.nc
     with (
         tc.tile_pool(name="keep", bufs=1) as keep,
-        tc.psum_pool(name="psum", bufs=PSUM_BANKS) as psum,
+        tc.psum_pool(name="psum", bufs=1) as psum,
         tc.manual_schedule(),
     ):
 
@@ -43,7 +49,7 @@ def tile_predictor_pb_v_kernel(tc, h, w2, b2, probs, grad_out, out):
         grad = per_pass([P, PACK, CLASSES], BF16, "grad")
         prob = per_pass([P, PACK, CLASSES], F32, "prob")
         hid = per_pass([P, PACK, CLASSES], BF16, "hid")
-        dz = per_pass([P, PACK + HALO, CLASSES], BF16, "dz")
+        dz = per_pass([P, PACK, CLASSES], BF16, "dz")
         neg_sum = per_pass([P, PACK], F32, "neg_sum")
         negated = per_pass([P, PACK, CLASSES], BF16, "negated")
         h_grouped = per_pass([P, CLASSES, PACK], BF16, "h_grouped")
@@ -53,141 +59,194 @@ def tile_predictor_pb_v_kernel(tc, h, w2, b2, probs, grad_out, out):
         dg_codes = [per_pass([P, CLASSES], U32, "dg_codes_%d" % s) for s in range(TAPS)]
         dg_scales = [per_pass([P, CLASSES], U8, "dg_scales_%d" % s) for s in range(TAPS)]
         result = [keep.tile([P, M_TILES, CLASSES], F32, name="result_%d" % s) for s in range(TAPS)]
+        edge_grad = keep.tile([P, PACK, CHUNK], BF16, name="edge_grad", align_bytes=64)
+        edge_prob = keep.tile([P, PACK, CHUNK], F32, name="edge_prob", align_bytes=64)
+        edge_part = keep.tile([P, PACK], F32, name="edge_part", align_bytes=64)
+        edge_dz = keep.tile([P, CHUNK, PACK], BF16, name="edge_dz", align_bytes=64)
+        minus_ones = keep.tile([P, P], F32, name="minus_ones", align_bytes=64)
+        shifter = keep.tile([P, 2 * P], BF16, name="shifter", align_bytes=64)
 
-        def load_rows(tiles, matrix, c, r0, r1):
-            nc.sync.dma_start(out=tiles[c][:, r0:r1, :], in_=rows_of_pass(matrix, c)[:, r0:r1, :])
+        a, b = 1, 0
+        half = CLASSES // 2
 
-        first, second = PASS_ORDER
-        for r0 in range(0, PACK, 2):
-            load_rows(grad, grad_out, first, r0, r0 + 2)
-            load_rows(prob, probs, first, r0, r0 + 1)
-            load_rows(prob, probs, first, r0 + 1, r0 + 2)
-        load_rows(grad, grad_out, second, 0, PACK)
-        nc.sync.dma_start(out=hid[first][:], in_=rows_of_pass(h, first))
-        for r0 in range(0, PACK, 2):
-            load_rows(prob, probs, second, r0, r0 + 2)
-        nc.sync.dma_start(out=hid[second][:], in_=rows_of_pass(h, second))
+        nc.gpsimd.memset(edge_grad[64:128, PACK - 1 : PACK, :], 0.0)
+        nc.gpsimd.memset(edge_prob[64:128, PACK - 1 : PACK, :], 0.0)
+        nc.gpsimd.memset(minus_ones[:], 0.0)
+        for q in range(PACK):
+            nc.gpsimd.memset(minus_ones[32 * q : 32 * q + 32, 32 * q : 32 * q + 32], -1.0)
+        nc.gpsimd.memset(shifter[:], 0.0)
+        make_identity(nc, shifter[:, 0:P])
 
-        nc.gpsimd.memset(dz[PASSES - 1][:, PACK : PACK + HALO, :], 0.0)
+        def load(tiles, matrix, c, t0, t1):
+            nc.sync.dma_start(out=tiles[c][:, t0:t1, :], in_=rows_of_pass(matrix, c)[:, t0:t1, :])
+
+        load(hid, h, a, 0, PACK)
+        for t0 in range(0, PACK, 2):
+            load(grad, grad_out, a, t0, t0 + 2)
+            load(prob, probs, a, t0, t0 + 1)
+            load(prob, probs, a, t0 + 1, t0 + 2)
+        for c in range(PASSES):
+            rows = slice(64 * c, 64 * c + 64)
+            j0, j1 = PACK * c + 1, min(PACK * c + 1 + PACK, TOKENS // P)
+            nc.sync.dma_start(out=edge_grad[rows, 0 : j1 - j0, :], in_=edge_rows(grad_out, j0, j1))
+            nc.sync.dma_start(out=edge_prob[rows, 0 : j1 - j0, :], in_=edge_rows(probs, j0, j1))
+        load(grad, grad_out, b, 0, PACK)
+        for t0 in range(0, PACK, 2):
+            load(prob, probs, b, t0, t0 + 2)
+        load(hid, h, b, 0, PACK)
 
         def negative_row_sums(c):
-            for r in range(PACK):
+            for t in range(PACK):
                 nc.scalar.activation(
-                    out=negated[c][:, r, :],
-                    in_=grad[c][:, r, :],
+                    out=negated[c][:, t, :],
+                    in_=grad[c][:, t, :],
                     func=mybir.ActivationFunctionType.Copy,
                     scale=-1.0,
-                    accum_out=neg_sum[c][:, r : r + 1],
+                    accum_out=neg_sum[c][:, t : t + 1],
                 )
 
-        def make_dz(c):
-            for r in range(PACK):
-                nc.vector.scalar_tensor_tensor(
-                    out=dz[c][:, r, :],
-                    in0=prob[c][:, r, :],
-                    scalar=neg_sum[c][:, r : r + 1],
-                    in1=grad[c][:, r, :],
-                    op0=mybir.AluOpType.mult,
-                    op1=mybir.AluOpType.add,
+        def dz_row(out_row, prob_row, minus_sum, grad_row):
+            nc.vector.scalar_tensor_tensor(
+                out=out_row,
+                in0=prob_row,
+                scalar=minus_sum,
+                in1=grad_row,
+                op0=mybir.AluOpType.mult,
+                op1=mybir.AluOpType.add,
+            )
+
+        def make_dz(c, *ts):
+            for t in ts:
+                dz_row(dz[c][:, t, :], prob[c][:, t, :], neg_sum[c][:, t : t + 1], grad[c][:, t, :])
+
+        def edge_sums():
+            nc.vector.tensor_reduce(
+                out=edge_part[:], in_=edge_grad[:], axis=mybir.AxisListType.X, op=mybir.AluOpType.add
+            )
+            total = psum.tile([P, PACK], F32, tag="bank7", name="edge_total")
+            nc.tensor.matmul(out=total[:], lhsT=minus_ones[:], rhs=edge_part[:], start=True, stop=True)
+            return total
+
+        def make_edge(total):
+            for t in range(PACK):
+                dz_row(edge_dz[:, :, t], edge_prob[:, t, :], total[:, t : t + 1], edge_grad[:, t, :])
+
+        def flat(tile):
+            return tile[:].rearrange("p w t -> p (w t)")
+
+        def place_edge(s, c):
+            for e in range(s):
+                p = P - s + e
+                q0 = 64 * c + 32 * e
+                nc.sync.dma_start(
+                    out=flat(dg_grouped[s][c])[p : p + 1, :], in_=flat(edge_dz)[q0 : q0 + CHUNKS, :]
                 )
 
-        def fetch_halo(c):
-            for lo, hi in ((0, P // 2), (P // 2, P - 1)):
-                nc.sync.dma_start(out=dz[c][lo:hi, PACK : PACK + HALO, :], in_=dz[c][lo + 1 : hi + 1, 0:HALO, :])
-            if c < PASSES - 1:
-                nc.sync.dma_start(out=dz[c][P - 1 : P, PACK : PACK + HALO, :], in_=dz[c + 1][0:1, 0:HALO, :])
+        def shift_by_dma(s, c):
+            for lo, hi in ((0, SPREAD), (SPREAD, P - s)):
+                nc.sync.dma_start(
+                    out=flat(dg_grouped[s][c])[lo:hi, :], in_=flat(dg_grouped[0][c])[lo + s : hi + s, :]
+                )
 
-        def regroup(copy, rows, grouped):
+        def shift_by_matmul(s, c, i, bank, copy):
+            width = half * PACK
+            moved = psum.tile([P, width], BF16, tag="bank%d" % bank, name="moved_%d_%d" % (s, i))
+            for n in range(0, width, 512):
+                nc.tensor.matmul(
+                    out=moved[:, n : n + 512],
+                    lhsT=shifter[:, s : s + P],
+                    rhs=flat(dg_grouped[0][c])[:, i * width + n : i * width + n + 512],
+                    start=True,
+                    stop=True,
+                )
+            copy(out=flat(dg_grouped[s][c])[0 : P - s, i * width : (i + 1) * width], in_=moved[0 : P - s, :])
+
+        def regroup(copy, rows, grouped, i):
+            cols = slice(i * half, (i + 1) * half)
             copy(
-                out=grouped[:].rearrange("p (c i) t -> p c t i", i=RUN),
-                in_=rows.rearrange("p t (c i) -> p c t i", i=RUN),
-            )
-
-        def quantise(grouped, packed_dtype, codes, scales):
-            nc.vector.quantize_mx(
-                out=codes[:].bitcast(packed_dtype),
-                scales=scales[:],
-                in_=grouped[:].rearrange("p w t -> p (w t)"),
-            )
-
-        def regroup_dg(copy, s, c):
-            regroup(copy, dz[c][:, s : s + PACK, :], dg_grouped[s][c])
-
-        def regroup_dg_half(s, c, w0):
-            cols = slice(w0, w0 + CLASSES // 2)
-            nc.vector.tensor_copy(
-                out=dg_grouped[s][c][:, cols, :].rearrange("p (c i) t -> p c t i", i=RUN),
-                in_=dz[c][:, s : s + PACK, cols].rearrange("p t (c i) -> p c t i", i=RUN),
-            )
-
-        def quantise_dg_half(s, c, w0):
-            cols = slice(w0, w0 + CLASSES // 2)
-            nc.vector.quantize_mx(
-                out=dg_codes[s][c][:, cols].bitcast(E5M2_X4),
-                scales=dg_scales[s][c][:, cols],
-                in_=dg_grouped[s][c][:, cols, :].rearrange("p w t -> p (w t)"),
+                out=grouped[:, cols, :].rearrange("p (c i) t -> p c t i", i=RUN),
+                in_=rows[:, :, cols].rearrange("p t (c i) -> p c t i", i=RUN),
             )
 
         def quantise_dg(s, c):
-            quantise(dg_grouped[s][c], E5M2_X4, dg_codes[s][c], dg_scales[s][c])
+            nc.vector.quantize_mx(
+                out=dg_codes[s][c][:].bitcast(E5M2_X4), scales=dg_scales[s][c][:], in_=flat(dg_grouped[s][c])
+            )
 
-        def quantise_h(c):
-            quantise(h_grouped[c], E4M3_X4, h_codes[c], h_scales[c])
+        def quantise_h(c, i):
+            cols = slice(i * half, (i + 1) * half)
+            nc.vector.quantize_mx(
+                out=h_codes[c][:, cols].bitcast(E4M3_X4),
+                scales=h_scales[c][:, cols],
+                in_=h_grouped[c][:, cols, :].rearrange("p w t -> p (w t)"),
+            )
 
         banks = {}
 
-        def multiply(s, c):
-            if c == PASS_ORDER[0]:
-                banks[s] = [psum.tile([P, CLASSES], F32, tag="bank", name="acc_%d_%d" % (s, m)) for m in range(M_TILES)]
-            for m in range(M_TILES):
+        def multiply(s, c, ms=tuple(range(M_TILES))):
+            for m in ms:
+                if c == a:
+                    banks[s, m] = psum.tile(
+                        [P, CLASSES], F32, tag="bank%d" % (M_TILES * (s % 2) + m), name="acc_%d_%d" % (s, m)
+                    )
                 m_cols = slice(m * P, (m + 1) * P)
                 nc.tensor.matmul_mx(
-                    out=banks[s][m][:],
+                    out=banks[s, m][:],
                     lhsT=h_codes[c][:, m_cols].bitcast(E4M3_X4),
                     lhsT_scale=h_scales[c][:, m_cols],
                     rhs=dg_codes[s][c][:].bitcast(E5M2_X4),
                     rhs_scale=dg_scales[s][c][:],
-                    start=(c == PASS_ORDER[0]),
-                    stop=(c == PASS_ORDER[-1]),
+                    start=(c == a),
+                    stop=(c == b),
                 )
 
-        def store(s, copies):
-            for m in range(M_TILES):
-                copies[m % len(copies)](out=result[s][:, m, :], in_=banks[s][m][:])
-                nc.sync.dma_start(out=out[TAPS - 1 - s, m * P : (m + 1) * P, :], in_=result[s][:, m, :])
+        def store(copy, s, m):
+            copy(out=result[s][:, m, :], in_=banks[s, m][:])
+            nc.sync.dma_start(out=out[TAPS - 1 - s, m * P : (m + 1) * P, :], in_=result[s][:, m, :])
 
         on_vector, on_scalar = nc.vector.tensor_copy, nc.scalar.copy
-        a, b = PASS_ORDER
+        regroup(on_vector, hid[a], h_grouped[a], 0)
+        regroup(on_scalar, hid[a], h_grouped[a], 1)
         negative_row_sums(a)
-        make_dz(a)
-        fetch_halo(a)
+        quantise_h(a, 0)
+        quantise_h(a, 1)
+        make_dz(a, 0, 1, 2)
+        total = edge_sums()
+        make_dz(a, 3)
         negative_row_sums(b)
-        regroup_dg(on_vector, 0, a)
+        make_edge(total)
+        regroup(on_vector, dz[a], dg_grouped[0][a], 0)
+        regroup(on_scalar, dz[a], dg_grouped[0][a], 1)
+        for s in (1, 2):
+            place_edge(s, a)
+            place_edge(s, b)
+        make_dz(b, 0, 1, 2, 3)
+        for s in (1, 2):
+            shift_by_dma(s, a)
         quantise_dg(0, a)
-        make_dz(b)
-        fetch_halo(b)
-        regroup(on_scalar, hid[a][:], h_grouped[a])
-        regroup(on_scalar, hid[b][:], h_grouped[b])
-        regroup_dg(on_scalar, 1, b)
-        regroup_dg(on_vector, 0, b)
-        quantise_h(a)
         multiply(0, a)
-        regroup_dg(on_vector, 1, a)
+        regroup(on_vector, dz[b], dg_grouped[0][b], 0)
+        regroup(on_vector, dz[b], dg_grouped[0][b], 1)
+        regroup(on_scalar, hid[b], h_grouped[b], 0)
+        regroup(on_scalar, hid[b], h_grouped[b], 1)
+        shift_by_dma(2, b)
+        quantise_h(b, 0)
         quantise_dg(0, b)
-        quantise_h(b)
+        quantise_h(b, 1)
+        shift_by_matmul(1, b, 0, 4, on_scalar)
+        shift_by_matmul(1, b, 1, 5, on_vector)
         multiply(0, b)
-        store(0, [on_scalar])
         quantise_dg(1, a)
-        multiply(1, a)
-        regroup_dg(on_vector, 2, a)
+        for m in range(M_TILES):
+            store(on_scalar, 0, m)
         quantise_dg(1, b)
+        multiply(1, a)
         multiply(1, b)
         quantise_dg(2, a)
+        quantise_dg(2, b)
         multiply(2, a)
-        regroup_dg_half(2, b, 0)
-        regroup_dg_half(2, b, CLASSES // 2)
-        quantise_dg_half(2, b, 0)
-        quantise_dg_half(2, b, CLASSES // 2)
+        for m in range(M_TILES):
+            store((on_scalar, on_vector)[m % 2], 1, m)
         multiply(2, b)
-        store(1, [on_scalar, on_scalar, on_scalar, on_vector])
-        store(2, [on_scalar, on_vector])
+        for m in range(M_TILES):
+            store((on_scalar, on_vector)[m % 2], 2, m)

@@ -15,10 +15,11 @@ P = 128
 PACK = 4
 K_PASS = P * PACK
 PASSES = TOKENS // K_PASS
-EDGE = TAPS - 1
+PAIR = 2
 CHUNK = 16
 CHUNKS = CLASSES // CHUNK
 M_TILES = CLASSES // P
+HALF = CLASSES // 2
 RUN = 4
 SPREAD = 112
 
@@ -27,12 +28,7 @@ BYTES = TOKENS * CLASSES * (2 + 2 + 4) + TAPS * CLASSES * CLASSES * 4
 
 
 def rows_of_pass(matrix, c):
-    return matrix[c * K_PASS : (c + 1) * K_PASS, :].rearrange("(t p) w -> p t w", p=P)
-
-
-def edge_rows(matrix, j0, j1):
-    rows = matrix[j0 * P : j1 * P, :].rearrange("(t p) w -> t p w", p=P)[:, 0:EDGE, :]
-    return rows.rearrange("t e (q i) -> (e q) t i", i=CHUNK)
+    return matrix[c * K_PASS : (c + 1) * K_PASS, :].rearrange("(u p e) w -> p u e w", u=PAIR, e=PAIR)
 
 
 def tile_predictor_pb_v_kernel(tc, h, w2, b2, probs, grad_out, out):
@@ -46,148 +42,154 @@ def tile_predictor_pb_v_kernel(tc, h, w2, b2, probs, grad_out, out):
         def per_pass(shape, dtype, name):
             return [keep.tile(shape, dtype, name="%s_%d" % (name, c), align_bytes=64) for c in range(PASSES)]
 
-        grad = per_pass([P, PACK, CLASSES], BF16, "grad")
-        prob = per_pass([P, PACK, CLASSES], F32, "prob")
-        hid = per_pass([P, PACK, CLASSES], BF16, "hid")
+        grad = per_pass([P, PAIR, PAIR, CLASSES], BF16, "grad")
+        prob = per_pass([P, PAIR, PAIR, CLASSES], F32, "prob")
+        hid = per_pass([P, PAIR, PAIR, CLASSES], BF16, "hid")
         dz = per_pass([P, PACK, CLASSES], BF16, "dz")
         neg_sum = per_pass([P, PACK], F32, "neg_sum")
         negated = per_pass([P, PACK, CLASSES], BF16, "negated")
         h_grouped = per_pass([P, CLASSES, PACK], BF16, "h_grouped")
         h_codes = per_pass([P, CLASSES], U32, "h_codes")
         h_scales = per_pass([P, CLASSES], U8, "h_scales")
-        dg_grouped = [per_pass([P, CLASSES, PACK], BF16, "dg_grouped_%d" % s) for s in range(TAPS)]
+        even = per_pass([P, PAIR, CLASSES, PACK], BF16, "even")
+        odd = per_pass([P, CLASSES, PACK], BF16, "odd")
         dg_codes = [per_pass([P, CLASSES], U32, "dg_codes_%d" % s) for s in range(TAPS)]
         dg_scales = [per_pass([P, CLASSES], U8, "dg_scales_%d" % s) for s in range(TAPS)]
         result = [keep.tile([P, M_TILES, CLASSES], F32, name="result_%d" % s) for s in range(TAPS)]
-        edge_grad = keep.tile([P, PACK, CHUNK], BF16, name="edge_grad", align_bytes=64)
-        edge_prob = keep.tile([P, PACK, CHUNK], F32, name="edge_prob", align_bytes=64)
-        edge_part = keep.tile([P, PACK], F32, name="edge_part", align_bytes=64)
-        edge_dz = keep.tile([P, CHUNK, PACK], BF16, name="edge_dz", align_bytes=64)
-        minus_ones = keep.tile([P, P], F32, name="minus_ones", align_bytes=64)
-        shifter = keep.tile([P, 2 * P], BF16, name="shifter", align_bytes=64)
+        edge_rows = per_pass([CHUNKS, PACK, CHUNK], BF16, "edge_rows")
+        edge = per_pass([CHUNKS, CHUNK, PACK], BF16, "edge")
+
+        one_down = keep.tile([P, 2 * P], BF16, name="one_down", align_bytes=64)
 
         a, b = 1, 0
-        half = CLASSES // 2
 
-        nc.gpsimd.memset(edge_grad[64:128, PACK - 1 : PACK, :], 0.0)
-        nc.gpsimd.memset(edge_prob[64:128, PACK - 1 : PACK, :], 0.0)
-        nc.gpsimd.memset(minus_ones[:], 0.0)
-        for q in range(PACK):
-            nc.gpsimd.memset(minus_ones[32 * q : 32 * q + 32, 32 * q : 32 * q + 32], -1.0)
-        nc.gpsimd.memset(shifter[:], 0.0)
-        make_identity(nc, shifter[:, 0:P])
+        nc.gpsimd.memset(edge_rows[a][:], 0.0)
+        nc.gpsimd.memset(one_down[:], 0.0)
+        make_identity(nc, one_down[:, 0:P])
 
-        def load(tiles, matrix, c, t0, t1):
-            nc.sync.dma_start(out=tiles[c][:, t0:t1, :], in_=rows_of_pass(matrix, c)[:, t0:t1, :])
+        def load(tiles, matrix, c, u):
+            nc.sync.dma_start(out=tiles[c][:, u, :, :], in_=rows_of_pass(matrix, c)[:, u, :, :])
 
-        load(hid, h, a, 0, PACK)
-        for t0 in range(0, PACK, 2):
-            load(grad, grad_out, a, t0, t0 + 2)
-            load(prob, probs, a, t0, t0 + 1)
-            load(prob, probs, a, t0 + 1, t0 + 2)
-        for c in range(PASSES):
-            rows = slice(64 * c, 64 * c + 64)
-            j0, j1 = PACK * c + 1, min(PACK * c + 1 + PACK, TOKENS // P)
-            nc.sync.dma_start(out=edge_grad[rows, 0 : j1 - j0, :], in_=edge_rows(grad_out, j0, j1))
-            nc.sync.dma_start(out=edge_prob[rows, 0 : j1 - j0, :], in_=edge_rows(probs, j0, j1))
-        load(grad, grad_out, b, 0, PACK)
-        for t0 in range(0, PACK, 2):
-            load(prob, probs, b, t0, t0 + 2)
-        load(hid, h, b, 0, PACK)
+        def load_row(tiles, matrix, c, u, e):
+            nc.sync.dma_start(out=tiles[c][:, u, e, :], in_=rows_of_pass(matrix, c)[:, u, e, :])
 
-        def negative_row_sums(c):
-            for t in range(PACK):
+        def load_all(tiles, matrix, c):
+            nc.sync.dma_start(out=tiles[c][:], in_=rows_of_pass(matrix, c))
+
+        load(grad, grad_out, a, 0)
+        load_row(prob, probs, a, 0, 0)
+        load_row(prob, probs, a, 0, 1)
+        load(grad, grad_out, a, 1)
+        load_row(prob, probs, a, 1, 0)
+        load_row(prob, probs, a, 1, 1)
+        load(grad, grad_out, b, 0)
+        load_all(hid, h, a)
+        load(prob, probs, b, 0)
+        load(grad, grad_out, b, 1)
+        load(prob, probs, b, 1)
+        load_all(hid, h, b)
+
+        def minus_row_sums(c, u):
+            for e in range(PAIR):
+                t = PAIR * e + u
                 nc.scalar.activation(
                     out=negated[c][:, t, :],
-                    in_=grad[c][:, t, :],
+                    in_=grad[c][:, u, e, :],
                     func=mybir.ActivationFunctionType.Copy,
                     scale=-1.0,
                     accum_out=neg_sum[c][:, t : t + 1],
                 )
 
-        def dz_row(out_row, prob_row, minus_sum, grad_row):
-            nc.vector.scalar_tensor_tensor(
-                out=out_row,
-                in0=prob_row,
-                scalar=minus_sum,
-                in1=grad_row,
-                op0=mybir.AluOpType.mult,
-                op1=mybir.AluOpType.add,
+        def make_dz(c, u):
+            for e in range(PAIR):
+                t = PAIR * e + u
+                nc.vector.scalar_tensor_tensor(
+                    out=dz[c][:, t, :],
+                    in0=prob[c][:, u, e, :],
+                    scalar=neg_sum[c][:, t : t + 1],
+                    in1=grad[c][:, u, e, :],
+                    op0=mybir.AluOpType.mult,
+                    op1=mybir.AluOpType.add,
+                )
+
+        def regroup_h(copy, c, i):
+            cols = slice(i * HALF, (i + 1) * HALF)
+            copy(
+                out=h_grouped[c][:, cols, :].rearrange("p (c i) (e u) -> p c e u i", i=RUN, u=PAIR),
+                in_=hid[c][:, :, :, cols].rearrange("p u e (c i) -> p c e u i", i=RUN),
             )
 
-        def make_dz(c, *ts):
-            for t in ts:
-                dz_row(dz[c][:, t, :], prob[c][:, t, :], neg_sum[c][:, t : t + 1], grad[c][:, t, :])
-
-        def edge_sums():
-            nc.vector.tensor_reduce(
-                out=edge_part[:], in_=edge_grad[:], axis=mybir.AxisListType.X, op=mybir.AluOpType.add
+        def regroup_dz(copy, c, i):
+            cols = slice(i * HALF, (i + 1) * HALF)
+            copy(
+                out=even[c][:, 0, cols, :].rearrange("p (c i) t -> p c t i", i=RUN),
+                in_=dz[c][:, :, cols].rearrange("p t (c i) -> p c t i", i=RUN),
             )
-            total = psum.tile([P, PACK], F32, tag="bank7", name="edge_total")
-            nc.tensor.matmul(out=total[:], lhsT=minus_ones[:], rhs=edge_part[:], start=True, stop=True)
-            return total
-
-        def make_edge(total):
-            for t in range(PACK):
-                dz_row(edge_dz[:, :, t], edge_prob[:, t, :], total[:, t : t + 1], edge_grad[:, t, :])
 
         def flat(tile):
-            return tile[:].rearrange("p w t -> p (w t)")
+            return tile.rearrange("p w t -> p (w t)")
 
-        def place_edge(s, c):
-            for e in range(s):
-                p = P - s + e
-                q0 = 64 * c + 32 * e
+        def shift_by_two(c):
+            for lo, hi in ((0, SPREAD), (SPREAD, P - 1)):
                 nc.sync.dma_start(
-                    out=flat(dg_grouped[s][c])[p : p + 1, :], in_=flat(edge_dz)[q0 : q0 + CHUNKS, :]
+                    out=flat(even[c][lo:hi, 1, :, :]), in_=flat(even[c][lo + 1 : hi + 1, 0, :, :])
                 )
 
-        def shift_by_dma(s, c):
-            for lo, hi in ((0, SPREAD), (SPREAD, P - s)):
-                nc.sync.dma_start(
-                    out=flat(dg_grouped[s][c])[lo:hi, :], in_=flat(dg_grouped[0][c])[lo + s : hi + s, :]
-                )
+        def fetch_edge(c, u, c_from):
+            for e in range(PAIR):
+                t = PAIR * e + u
+                row = dz[c_from][0:1, t + 1 - 2 * u, :]
+                nc.sync.dma_start(out=edge_rows[c][:, t, :], in_=row.rearrange("o (q i) -> o q i", i=CHUNK))
 
-        def shift_by_matmul(s, c, i, bank, copy):
-            width = half * PACK
-            moved = psum.tile([P, width], BF16, tag="bank%d" % bank, name="moved_%d_%d" % (s, i))
-            for n in range(0, width, 512):
+        def place_edge(c):
+            nc.vector.tensor_copy(out=edge[c][:], in_=edge_rows[c][:].rearrange("q t i -> q i t"))
+            nc.sync.dma_start(out=flat(even[c][P - 1 : P, 1, :, :]), in_=flat(edge[c][:]))
+
+        def shift_by_one(copy, c):
+            words = even[c][:].rearrange("p a w t -> p (a w t)").bitcast(F32)
+            tile_words = CLASSES * PAIR
+            pairs = words[:, 1 : 2 * tile_words - 1].rearrange("p (j x) -> p j x", j=PAIR)
+            copy(
+                out=flat(odd[c][:]).bitcast(F32).rearrange("p (w j) -> p w j", j=PAIR),
+                in_=pairs[:, :, 0 : tile_words - 1 : PAIR].rearrange("p j w -> p w j"),
+            )
+
+        def shift_by_two_on_tensor(copy, c, i, bank):
+            cols = slice(i * HALF, (i + 1) * HALF)
+            moved = psum.tile([P, HALF * PACK], BF16, tag="bank%d" % bank, name="moved_%d" % i)
+            for n in range(0, HALF * PACK, CLASSES):
                 nc.tensor.matmul(
-                    out=moved[:, n : n + 512],
-                    lhsT=shifter[:, s : s + P],
-                    rhs=flat(dg_grouped[0][c])[:, i * width + n : i * width + n + 512],
+                    out=moved[:, n : n + CLASSES],
+                    lhsT=one_down[:, 1 : 1 + P],
+                    rhs=flat(even[c][:, 0, cols, :])[:, n : n + CLASSES],
                     start=True,
                     stop=True,
                 )
-            copy(out=flat(dg_grouped[s][c])[0 : P - s, i * width : (i + 1) * width], in_=moved[0 : P - s, :])
+            copy(out=flat(even[c][0 : P - 1, 1, cols, :]), in_=moved[0 : P - 1, :])
 
-        def regroup(copy, rows, grouped, i):
-            cols = slice(i * half, (i + 1) * half)
-            copy(
-                out=grouped[:, cols, :].rearrange("p (c i) t -> p c t i", i=RUN),
-                in_=rows[:, :, cols].rearrange("p t (c i) -> p c t i", i=RUN),
-            )
+        def shifted(s, c):
+            return flat(odd[c][:]) if s == 1 else flat(even[c][:, s // 2, :, :])
 
         def quantise_dg(s, c):
             nc.vector.quantize_mx(
-                out=dg_codes[s][c][:].bitcast(E5M2_X4), scales=dg_scales[s][c][:], in_=flat(dg_grouped[s][c])
+                out=dg_codes[s][c][:].bitcast(E5M2_X4), scales=dg_scales[s][c][:], in_=shifted(s, c)
             )
 
         def quantise_h(c, i):
-            cols = slice(i * half, (i + 1) * half)
+            cols = slice(i * HALF, (i + 1) * HALF)
             nc.vector.quantize_mx(
                 out=h_codes[c][:, cols].bitcast(E4M3_X4),
                 scales=h_scales[c][:, cols],
-                in_=h_grouped[c][:, cols, :].rearrange("p w t -> p (w t)"),
+                in_=flat(h_grouped[c][:, cols, :]),
             )
 
         banks = {}
 
-        def multiply(s, c, ms=tuple(range(M_TILES))):
+        def multiply(s, c, *ms):
             for m in ms:
                 if c == a:
                     banks[s, m] = psum.tile(
-                        [P, CLASSES], F32, tag="bank%d" % (M_TILES * (s % 2) + m), name="acc_%d_%d" % (s, m)
+                        [P, CLASSES], F32, tag="bank%d" % (M_TILES * (s // 2) + m), name="acc_%d_%d" % (s, m)
                     )
                 m_cols = slice(m * P, (m + 1) * P)
                 nc.tensor.matmul_mx(
@@ -205,48 +207,59 @@ def tile_predictor_pb_v_kernel(tc, h, w2, b2, probs, grad_out, out):
             nc.sync.dma_start(out=out[TAPS - 1 - s, m * P : (m + 1) * P, :], in_=result[s][:, m, :])
 
         on_vector, on_scalar = nc.vector.tensor_copy, nc.scalar.copy
-        regroup(on_vector, hid[a], h_grouped[a], 0)
-        regroup(on_scalar, hid[a], h_grouped[a], 1)
-        negative_row_sums(a)
-        quantise_h(a, 0)
-        quantise_h(a, 1)
-        make_dz(a, 0, 1, 2)
-        total = edge_sums()
-        make_dz(a, 3)
-        negative_row_sums(b)
-        make_edge(total)
-        regroup(on_vector, dz[a], dg_grouped[0][a], 0)
-        regroup(on_scalar, dz[a], dg_grouped[0][a], 1)
-        for s in (1, 2):
-            place_edge(s, a)
-            place_edge(s, b)
-        make_dz(b, 0, 1, 2, 3)
-        for s in (1, 2):
-            shift_by_dma(s, a)
+        minus_row_sums(a, 0)
+        make_dz(a, 0)
+        minus_row_sums(a, 1)
+        make_dz(a, 1)
+        fetch_edge(a, 0, a)
+        fetch_edge(b, 1, a)
+        minus_row_sums(b, 0)
+        regroup_dz(on_vector, a, 0)
+        regroup_dz(on_vector, a, 1)
+        shift_by_two(a)
+        regroup_h(on_scalar, a, 0)
+        minus_row_sums(b, 1)
         quantise_dg(0, a)
-        multiply(0, a)
-        regroup(on_vector, dz[b], dg_grouped[0][b], 0)
-        regroup(on_vector, dz[b], dg_grouped[0][b], 1)
-        regroup(on_scalar, hid[b], h_grouped[b], 0)
-        regroup(on_scalar, hid[b], h_grouped[b], 1)
-        shift_by_dma(2, b)
-        quantise_h(b, 0)
+        make_dz(b, 0)
+        quantise_h(a, 0)
+        multiply(0, a, 0, 1)
+        regroup_h(on_scalar, a, 1)
+        make_dz(b, 1)
+        fetch_edge(b, 0, b)
+        quantise_h(a, 1)
+        multiply(0, a, 2, 3)
+        regroup_dz(on_vector, b, 0)
+        regroup_dz(on_scalar, b, 1)
+        place_edge(a)
+        regroup_h(on_vector, b, 0)
+        regroup_h(on_scalar, b, 1)
+        shift_by_two_on_tensor(on_scalar, b, 0, 4)
+        shift_by_two_on_tensor(on_scalar, b, 1, 5)
         quantise_dg(0, b)
+        quantise_h(b, 0)
+        multiply(0, b, 0, 1)
+        place_edge(b)
         quantise_h(b, 1)
-        shift_by_matmul(1, b, 0, 4, on_scalar)
-        shift_by_matmul(1, b, 1, 5, on_vector)
-        multiply(0, b)
-        quantise_dg(1, a)
-        for m in range(M_TILES):
-            store(on_scalar, 0, m)
-        quantise_dg(1, b)
-        multiply(1, a)
-        multiply(1, b)
+        multiply(0, b, 2, 3)
         quantise_dg(2, a)
+        store(on_scalar, 0, 0)
+        store(on_vector, 0, 1)
+        store(on_scalar, 0, 2)
+        store(on_vector, 0, 3)
+        multiply(2, a, 0, 1, 2, 3)
         quantise_dg(2, b)
-        multiply(2, a)
-        for m in range(M_TILES):
-            store((on_scalar, on_vector)[m % 2], 1, m)
-        multiply(2, b)
-        for m in range(M_TILES):
-            store((on_scalar, on_vector)[m % 2], 2, m)
+        multiply(2, b, 0, 1, 2, 3)
+        shift_by_one(on_scalar, b)
+        shift_by_one(on_vector, a)
+        store(on_scalar, 2, 0)
+        store(on_scalar, 2, 1)
+        store(on_scalar, 2, 2)
+        quantise_dg(1, b)
+        quantise_dg(1, a)
+        store(on_vector, 2, 3)
+        multiply(1, a, 0, 1, 2, 3)
+        multiply(1, b, 0, 1, 2, 3)
+        store(on_scalar, 1, 0)
+        store(on_vector, 1, 1)
+        store(on_scalar, 1, 2)
+        store(on_vector, 1, 3)

@@ -1,5 +1,4 @@
 import concourse.mybir as mybir
-from concourse.masks import make_identity
 
 BF16 = mybir.dt.bfloat16
 F32 = mybir.dt.float32
@@ -20,6 +19,7 @@ CHUNK = 16
 CHUNKS = CLASSES // CHUNK
 M_TILES = CLASSES // P
 HALF = CLASSES // 2
+ALL, LEFT, RIGHT = slice(0, CLASSES), slice(0, HALF), slice(HALF, CLASSES)
 RUN = 4
 SPREAD = 112
 
@@ -59,13 +59,10 @@ def tile_predictor_pb_v_kernel(tc, h, w2, b2, probs, grad_out, out):
         edge_rows = per_pass([CHUNKS, PACK, CHUNK], BF16, "edge_rows")
         edge = per_pass([CHUNKS, CHUNK, PACK], BF16, "edge")
 
-        one_down = keep.tile([P, 2 * P], BF16, name="one_down", align_bytes=64)
 
         a, b = 1, 0
 
         nc.gpsimd.memset(edge_rows[a][:], 0.0)
-        nc.gpsimd.memset(one_down[:], 0.0)
-        make_identity(nc, one_down[:, 0:P])
 
         def load(tiles, matrix, c, u):
             nc.sync.dma_start(out=tiles[c][:, u, :, :], in_=rows_of_pass(matrix, c)[:, u, :, :])
@@ -76,18 +73,17 @@ def tile_predictor_pb_v_kernel(tc, h, w2, b2, probs, grad_out, out):
         def load_all(tiles, matrix, c):
             nc.sync.dma_start(out=tiles[c][:], in_=rows_of_pass(matrix, c))
 
-        load(grad, grad_out, a, 0)
-        load_row(prob, probs, a, 0, 0)
-        load_row(prob, probs, a, 0, 1)
         load(grad, grad_out, a, 1)
         load_row(prob, probs, a, 1, 0)
+        load(grad, grad_out, a, 0)
         load_row(prob, probs, a, 1, 1)
-        load(grad, grad_out, b, 0)
-        load_all(hid, h, a)
-        load(prob, probs, b, 0)
         load(grad, grad_out, b, 1)
+        load(grad, grad_out, b, 0)
+        load_row(prob, probs, a, 0, 0)
+        load_row(prob, probs, a, 0, 1)
         load(prob, probs, b, 1)
-        load_all(hid, h, b)
+        load(prob, probs, b, 0)
+        load_all(hid, h, a)
 
         def minus_row_sums(c, u):
             for e in range(PAIR):
@@ -112,15 +108,13 @@ def tile_predictor_pb_v_kernel(tc, h, w2, b2, probs, grad_out, out):
                     op1=mybir.AluOpType.add,
                 )
 
-        def regroup_h(copy, c, i):
-            cols = slice(i * HALF, (i + 1) * HALF)
+        def regroup_h(copy, c, cols):
             copy(
                 out=h_grouped[c][:, cols, :].rearrange("p (c i) (e u) -> p c e u i", i=RUN, u=PAIR),
                 in_=hid[c][:, :, :, cols].rearrange("p u e (c i) -> p c e u i", i=RUN),
             )
 
-        def regroup_dz(copy, c, i):
-            cols = slice(i * HALF, (i + 1) * HALF)
+        def regroup_dz(copy, c, cols):
             copy(
                 out=even[c][:, 0, cols, :].rearrange("p (c i) t -> p c t i", i=RUN),
                 in_=dz[c][:, :, cols].rearrange("p t (c i) -> p c t i", i=RUN),
@@ -154,19 +148,6 @@ def tile_predictor_pb_v_kernel(tc, h, w2, b2, probs, grad_out, out):
                 in_=pairs[:, :, 0 : tile_words - 1 : PAIR].rearrange("p j w -> p w j"),
             )
 
-        def shift_by_two_on_tensor(copy, c, i, bank):
-            cols = slice(i * HALF, (i + 1) * HALF)
-            moved = psum.tile([P, HALF * PACK], BF16, tag="bank%d" % bank, name="moved_%d" % i)
-            for n in range(0, HALF * PACK, CLASSES):
-                nc.tensor.matmul(
-                    out=moved[:, n : n + CLASSES],
-                    lhsT=one_down[:, 1 : 1 + P],
-                    rhs=flat(even[c][:, 0, cols, :])[:, n : n + CLASSES],
-                    start=True,
-                    stop=True,
-                )
-            copy(out=flat(even[c][0 : P - 1, 1, cols, :]), in_=moved[0 : P - 1, :])
-
         def shifted(s, c):
             return flat(odd[c][:]) if s == 1 else flat(even[c][:, s // 2, :, :])
 
@@ -175,8 +156,7 @@ def tile_predictor_pb_v_kernel(tc, h, w2, b2, probs, grad_out, out):
                 out=dg_codes[s][c][:].bitcast(E5M2_X4), scales=dg_scales[s][c][:], in_=shifted(s, c)
             )
 
-        def quantise_h(c, i):
-            cols = slice(i * HALF, (i + 1) * HALF)
+        def quantise_h(c, cols):
             nc.vector.quantize_mx(
                 out=h_codes[c][:, cols].bitcast(E4M3_X4),
                 scales=h_scales[c][:, cols],
@@ -207,59 +187,52 @@ def tile_predictor_pb_v_kernel(tc, h, w2, b2, probs, grad_out, out):
             nc.sync.dma_start(out=out[TAPS - 1 - s, m * P : (m + 1) * P, :], in_=result[s][:, m, :])
 
         on_vector, on_scalar = nc.vector.tensor_copy, nc.scalar.copy
-        minus_row_sums(a, 0)
-        make_dz(a, 0)
         minus_row_sums(a, 1)
+        minus_row_sums(a, 0)
+        minus_row_sums(b, 1)
+        minus_row_sums(b, 0)
         make_dz(a, 1)
+        make_dz(a, 0)
         fetch_edge(a, 0, a)
         fetch_edge(b, 1, a)
-        minus_row_sums(b, 0)
-        regroup_dz(on_vector, a, 0)
-        regroup_dz(on_vector, a, 1)
-        shift_by_two(a)
-        regroup_h(on_scalar, a, 0)
-        minus_row_sums(b, 1)
-        quantise_dg(0, a)
-        make_dz(b, 0)
-        quantise_h(a, 0)
-        multiply(0, a, 0, 1)
-        regroup_h(on_scalar, a, 1)
+        load_all(hid, h, b)
         make_dz(b, 1)
+        make_dz(b, 0)
         fetch_edge(b, 0, b)
-        quantise_h(a, 1)
-        multiply(0, a, 2, 3)
-        regroup_dz(on_vector, b, 0)
-        regroup_dz(on_scalar, b, 1)
+        regroup_dz(on_scalar, a, ALL)
+        regroup_dz(on_scalar, b, LEFT)
+        regroup_dz(on_vector, b, RIGHT)
+        shift_by_two(a)
+        quantise_dg(0, a)
         place_edge(a)
-        regroup_h(on_vector, b, 0)
-        regroup_h(on_scalar, b, 1)
-        shift_by_two_on_tensor(on_scalar, b, 0, 4)
-        shift_by_two_on_tensor(on_scalar, b, 1, 5)
+        regroup_h(on_vector, a, LEFT)
+        shift_by_two(b)
         quantise_dg(0, b)
-        quantise_h(b, 0)
-        multiply(0, b, 0, 1)
         place_edge(b)
-        quantise_h(b, 1)
+        quantise_h(a, LEFT)
+        regroup_h(on_vector, b, LEFT)
+        regroup_h(on_scalar, a, RIGHT)
+        regroup_h(on_scalar, b, RIGHT)
+        quantise_h(b, LEFT)
+        multiply(0, a, 0, 1)
+        multiply(0, b, 0, 1)
+        quantise_h(a, RIGHT)
+        quantise_h(b, RIGHT)
+        multiply(0, a, 2, 3)
         multiply(0, b, 2, 3)
+        for m in range(M_TILES):
+            store(on_scalar, 0, m)
         quantise_dg(2, a)
-        store(on_scalar, 0, 0)
-        store(on_vector, 0, 1)
-        store(on_scalar, 0, 2)
-        store(on_vector, 0, 3)
-        multiply(2, a, 0, 1, 2, 3)
         quantise_dg(2, b)
+        multiply(2, a, 0, 1, 2, 3)
         multiply(2, b, 0, 1, 2, 3)
-        shift_by_one(on_scalar, b)
+        for m in range(M_TILES):
+            store(on_scalar, 2, m)
         shift_by_one(on_vector, a)
-        store(on_scalar, 2, 0)
-        store(on_scalar, 2, 1)
-        store(on_scalar, 2, 2)
-        quantise_dg(1, b)
+        shift_by_one(on_vector, b)
         quantise_dg(1, a)
-        store(on_vector, 2, 3)
+        quantise_dg(1, b)
         multiply(1, a, 0, 1, 2, 3)
         multiply(1, b, 0, 1, 2, 3)
-        store(on_scalar, 1, 0)
-        store(on_vector, 1, 1)
-        store(on_scalar, 1, 2)
-        store(on_vector, 1, 3)
+        for m in range(M_TILES):
+            store((on_scalar, on_vector)[m % 2], 1, m)

@@ -21,7 +21,7 @@ M_TILES = CLASSES // P
 HALF = CLASSES // 2
 ALL, LEFT, RIGHT = slice(0, CLASSES), slice(0, HALF), slice(HALF, CLASSES)
 RUN = 4
-SPREAD = 112
+SHIFT_CUTS = (0, 126, P - 1)
 
 FLOPS = 2 * TAPS * TOKENS * CLASSES * CLASSES
 BYTES = TOKENS * CLASSES * (2 + 2 + 4) + TAPS * CLASSES * CLASSES * 4
@@ -124,7 +124,7 @@ def tile_predictor_pb_v_kernel(tc, h, w2, b2, probs, grad_out, out):
             return tile.rearrange("p w t -> p (w t)")
 
         def shift_by_two(c):
-            for lo, hi in ((0, SPREAD), (SPREAD, P - 1)):
+            for lo, hi in zip(SHIFT_CUTS, SHIFT_CUTS[1:]):
                 nc.sync.dma_start(
                     out=flat(even[c][lo:hi, 1, :, :]), in_=flat(even[c][lo + 1 : hi + 1, 0, :, :])
                 )
@@ -136,7 +136,7 @@ def tile_predictor_pb_v_kernel(tc, h, w2, b2, probs, grad_out, out):
                 nc.sync.dma_start(out=edge_rows[c][:, t, :], in_=row.rearrange("o (q i) -> o q i", i=CHUNK))
 
         def place_edge(c):
-            nc.vector.tensor_copy(out=edge[c][:], in_=edge_rows[c][:].rearrange("q t i -> q i t"))
+            nc.gpsimd.tensor_copy(out=edge[c][:], in_=edge_rows[c][:].rearrange("q t i -> q i t"))
             nc.sync.dma_start(out=flat(even[c][P - 1 : P, 1, :, :]), in_=flat(edge[c][:]))
 
         def shift_by_one(copy, c):
@@ -204,10 +204,10 @@ def tile_predictor_pb_v_kernel(tc, h, w2, b2, probs, grad_out, out):
         regroup_dz(on_vector, b, RIGHT)
         shift_by_two(a)
         quantise_dg(0, a)
-        place_edge(a)
         regroup_h(on_vector, a, LEFT)
         shift_by_two(b)
         quantise_dg(0, b)
+        place_edge(a)
         place_edge(b)
         quantise_h(a, LEFT)
         regroup_h(on_vector, b, LEFT)
@@ -224,15 +224,17 @@ def tile_predictor_pb_v_kernel(tc, h, w2, b2, probs, grad_out, out):
             store(on_scalar, 0, m)
         quantise_dg(2, a)
         quantise_dg(2, b)
-        multiply(2, a, 0, 1, 2, 3)
-        multiply(2, b, 0, 1, 2, 3)
+        for m in range(0, M_TILES, 2):
+            multiply(2, a, m, m + 1)
+            multiply(2, b, m, m + 1)
         for m in range(M_TILES):
             store(on_scalar, 2, m)
         shift_by_one(on_vector, a)
         shift_by_one(on_vector, b)
         quantise_dg(1, a)
         quantise_dg(1, b)
-        multiply(1, a, 0, 1, 2, 3)
-        multiply(1, b, 0, 1, 2, 3)
+        for m in range(0, M_TILES, 2):
+            multiply(1, a, m, m + 1)
+            multiply(1, b, m, m + 1)
         for m in range(M_TILES):
             store((on_scalar, on_vector)[m % 2], 1, m)

@@ -1,4 +1,5 @@
 import concourse.mybir as mybir
+from concourse.masks import make_identity
 
 BF16 = mybir.dt.bfloat16
 F32 = mybir.dt.float32
@@ -59,10 +60,13 @@ def tile_predictor_pb_v_kernel(tc, h, w2, b2, probs, grad_out, out):
         edge_rows = per_pass([CHUNKS, PACK, CHUNK], BF16, "edge_rows")
         edge = per_pass([CHUNKS, CHUNK, PACK], BF16, "edge")
 
+        one_down = keep.tile([P, 2 * P], BF16, name="one_down", align_bytes=64)
 
         a, b = 1, 0
 
         nc.gpsimd.memset(edge_rows[a][:], 0.0)
+        nc.gpsimd.memset(one_down[:], 0.0)
+        make_identity(nc, one_down[:, 0:P])
 
         def load(tiles, matrix, c, u):
             nc.sync.dma_start(out=tiles[c][:, u, :, :], in_=rows_of_pass(matrix, c)[:, u, :, :])
@@ -144,9 +148,24 @@ def tile_predictor_pb_v_kernel(tc, h, w2, b2, probs, grad_out, out):
             tile_words = CLASSES * PAIR
             pairs = words[:, 1 : 2 * tile_words - 1].rearrange("p (j x) -> p j x", j=PAIR)
             copy(
-                out=flat(odd[c][:]).bitcast(F32).rearrange("p (w j) -> p w j", j=PAIR),
-                in_=pairs[:, :, 0 : tile_words - 1 : PAIR].rearrange("p j w -> p w j"),
+                out=flat(odd[c][:]).bitcast(F32).rearrange("p (c i j) -> p c j i", i=RUN, j=PAIR),
+                in_=pairs[:, :, 0 : tile_words - 1 : PAIR].rearrange("p j (c i) -> p c j i", i=RUN),
             )
+
+        def move_down(c, cols, bank):
+            moved = psum.tile([P, HALF * PACK], BF16, tag="bank%d" % bank, name="moved_%d" % bank)
+            for n in range(0, HALF * PACK, CLASSES):
+                nc.tensor.matmul(
+                    out=moved[:, n : n + CLASSES],
+                    lhsT=one_down[:, 1 : 1 + P],
+                    rhs=flat(even[c][:, 0, cols, :])[:, n : n + CLASSES],
+                    start=True,
+                    stop=True,
+                )
+            return moved
+
+        def fetch_moved(copy, c, cols, moved):
+            copy(out=flat(even[c][0 : P - 1, 1, cols, :]), in_=moved[0 : P - 1, :])
 
         def shifted(s, c):
             return flat(odd[c][:]) if s == 1 else flat(even[c][:, s // 2, :, :])
@@ -202,12 +221,13 @@ def tile_predictor_pb_v_kernel(tc, h, w2, b2, probs, grad_out, out):
         regroup_dz(on_scalar, a, ALL)
         regroup_dz(on_scalar, b, LEFT)
         regroup_dz(on_vector, b, RIGHT)
+        moved_right = move_down(b, RIGHT, 4)
+        moved_left = move_down(b, LEFT, 5)
         shift_by_two(a)
+        place_edge(a)
         quantise_dg(0, a)
         regroup_h(on_vector, a, LEFT)
-        shift_by_two(b)
         quantise_dg(0, b)
-        place_edge(a)
         place_edge(b)
         quantise_h(a, LEFT)
         regroup_h(on_vector, b, LEFT)
@@ -220,6 +240,8 @@ def tile_predictor_pb_v_kernel(tc, h, w2, b2, probs, grad_out, out):
         quantise_h(b, RIGHT)
         multiply(0, a, 2, 3)
         multiply(0, b, 2, 3)
+        fetch_moved(on_scalar, b, LEFT, moved_left)
+        fetch_moved(on_vector, b, RIGHT, moved_right)
         for m in range(M_TILES):
             store(on_scalar, 0, m)
         quantise_dg(2, a)

@@ -82,12 +82,13 @@ def tile_predictor_pb_v_kernel(tc, h, w2, b2, probs, grad_out, out):
         load(grad, grad_out, a, 0)
         load_row(prob, probs, a, 1, 1)
         load(grad, grad_out, b, 1)
-        load(grad, grad_out, b, 0)
         load_row(prob, probs, a, 0, 0)
         load_row(prob, probs, a, 0, 1)
-        load(prob, probs, b, 1)
-        load(prob, probs, b, 0)
+        load_row(prob, probs, b, 1, 0)
         load_all(hid, h, a)
+        load(grad, grad_out, b, 0)
+        load_row(prob, probs, b, 1, 1)
+        load(prob, probs, b, 0)
 
         def minus_row_sums(c, u):
             for e in range(PAIR):
@@ -100,17 +101,20 @@ def tile_predictor_pb_v_kernel(tc, h, w2, b2, probs, grad_out, out):
                     accum_out=neg_sum[c][:, t : t + 1],
                 )
 
+        def make_dz_row(c, u, e):
+            t = PAIR * e + u
+            nc.vector.scalar_tensor_tensor(
+                out=dz[c][:, t, :],
+                in0=prob[c][:, u, e, :],
+                scalar=neg_sum[c][:, t : t + 1],
+                in1=grad[c][:, u, e, :],
+                op0=mybir.AluOpType.mult,
+                op1=mybir.AluOpType.add,
+            )
+
         def make_dz(c, u):
             for e in range(PAIR):
-                t = PAIR * e + u
-                nc.vector.scalar_tensor_tensor(
-                    out=dz[c][:, t, :],
-                    in0=prob[c][:, u, e, :],
-                    scalar=neg_sum[c][:, t : t + 1],
-                    in1=grad[c][:, u, e, :],
-                    op0=mybir.AluOpType.mult,
-                    op1=mybir.AluOpType.add,
-                )
+                make_dz_row(c, u, e)
 
         def regroup_h(copy, c, cols):
             copy(
@@ -209,46 +213,49 @@ def tile_predictor_pb_v_kernel(tc, h, w2, b2, probs, grad_out, out):
         minus_row_sums(a, 1)
         minus_row_sums(a, 0)
         minus_row_sums(b, 1)
-        minus_row_sums(b, 0)
         make_dz(a, 1)
         make_dz(a, 0)
         fetch_edge(a, 0, a)
         fetch_edge(b, 1, a)
         load_all(hid, h, b)
-        make_dz(b, 1)
+        make_dz_row(b, 1, 0)
+        regroup_dz(on_vector, a, LEFT)
+        regroup_dz(on_scalar, a, RIGHT)
+        shift_by_two(a)
+        regroup_h(on_vector, a, LEFT)
+        regroup_h(on_scalar, a, RIGHT)
+        quantise_dg(0, a)
+        minus_row_sums(b, 0)
+        make_dz_row(b, 1, 1)
+        quantise_h(a, LEFT)
+        multiply(0, a, 0, 1)
         make_dz(b, 0)
         fetch_edge(b, 0, b)
-        regroup_dz(on_scalar, a, ALL)
-        regroup_dz(on_scalar, b, LEFT)
+        quantise_h(a, RIGHT)
+        multiply(0, a, 2, 3)
+        regroup_dz(on_vector, b, LEFT)
         regroup_dz(on_vector, b, RIGHT)
-        moved_right = move_down(b, RIGHT, 4)
-        moved_left = move_down(b, LEFT, 5)
-        shift_by_two(a)
+        moved_left = move_down(b, LEFT, 4)
+        moved_right = move_down(b, RIGHT, 5)
         place_edge(a)
-        quantise_dg(0, a)
-        regroup_h(on_vector, a, LEFT)
-        quantise_dg(0, b)
-        place_edge(b)
-        quantise_h(a, LEFT)
-        regroup_h(on_vector, b, LEFT)
-        regroup_h(on_scalar, a, RIGHT)
+        regroup_h(on_scalar, b, LEFT)
         regroup_h(on_scalar, b, RIGHT)
         quantise_h(b, LEFT)
-        multiply(0, a, 0, 1)
+        quantise_dg(0, b)
+        place_edge(b)
         multiply(0, b, 0, 1)
-        quantise_h(a, RIGHT)
         quantise_h(b, RIGHT)
-        multiply(0, a, 2, 3)
         multiply(0, b, 2, 3)
-        fetch_moved(on_scalar, b, LEFT, moved_left)
-        fetch_moved(on_vector, b, RIGHT, moved_right)
+        fetch_moved(on_scalar, b, RIGHT, moved_right)
         for m in range(M_TILES):
             store(on_scalar, 0, m)
         quantise_dg(2, a)
+        fetch_moved(on_vector, b, LEFT, moved_left)
         quantise_dg(2, b)
-        for m in range(0, M_TILES, 2):
-            multiply(2, a, m, m + 1)
-            multiply(2, b, m, m + 1)
+        multiply(2, a, 0, 1, 2)
+        multiply(2, b, 0, 1)
+        multiply(2, a, 3)
+        multiply(2, b, 2, 3)
         for m in range(M_TILES):
             store(on_scalar, 2, m)
         shift_by_one(on_vector, a)
@@ -259,4 +266,4 @@ def tile_predictor_pb_v_kernel(tc, h, w2, b2, probs, grad_out, out):
             multiply(1, a, m, m + 1)
             multiply(1, b, m, m + 1)
         for m in range(M_TILES):
-            store((on_scalar, on_vector)[m % 2], 1, m)
+            store((on_vector, on_scalar)[m % 2], 1, m)

import concourse.mybir as mybir
from concourse.masks import make_identity

BF16 = mybir.dt.bfloat16
F32 = mybir.dt.float32
U32 = mybir.dt.uint32
U8 = mybir.dt.uint8
E4M3_X4 = mybir.dt.float8_e4m3fn_x4
E5M2_X4 = mybir.dt.float8_e5m2_x4

TOKENS = 1024
CLASSES = 512
TAPS = 3
P = 128
PACK = 4
K_PASS = P * PACK
PASSES = TOKENS // K_PASS
PAIR = 2
CHUNK = 16
CHUNKS = CLASSES // CHUNK
M_TILES = CLASSES // P
HALF = CLASSES // 2
ALL, LEFT, RIGHT = slice(0, CLASSES), slice(0, HALF), slice(HALF, CLASSES)
RUN = 4
SHIFT_CUTS = (0, 126, P - 1)

FLOPS = 2 * TAPS * TOKENS * CLASSES * CLASSES
BYTES = TOKENS * CLASSES * (2 + 2 + 4) + TAPS * CLASSES * CLASSES * 4


def rows_of_pass(matrix, c):
    return matrix[c * K_PASS : (c + 1) * K_PASS, :].rearrange("(u p e) w -> p u e w", u=PAIR, e=PAIR)


def tile_predictor_pb_v_kernel(tc, h, w2, b2, probs, grad_out, out):
    nc = tc.nc
    with (
        tc.tile_pool(name="keep", bufs=1) as keep,
        tc.psum_pool(name="psum", bufs=1) as psum,
        tc.manual_schedule(),
    ):

        def per_pass(shape, dtype, name):
            return [keep.tile(shape, dtype, name="%s_%d" % (name, c), align_bytes=64) for c in range(PASSES)]

        grad = per_pass([P, PAIR, PAIR, CLASSES], BF16, "grad")
        prob = per_pass([P, PAIR, PAIR, CLASSES], F32, "prob")
        hid = per_pass([P, PAIR, PAIR, CLASSES], BF16, "hid")
        dz = per_pass([P, PACK, CLASSES], BF16, "dz")
        neg_sum = per_pass([P, PACK], F32, "neg_sum")
        negated = per_pass([P, PACK, CLASSES], BF16, "negated")
        h_grouped = per_pass([P, CLASSES, PACK], BF16, "h_grouped")
        h_codes = per_pass([P, CLASSES], U32, "h_codes")
        h_scales = per_pass([P, CLASSES], U8, "h_scales")
        even = per_pass([P, PAIR, CLASSES, PACK], BF16, "even")
        odd = per_pass([P, CLASSES, PACK], BF16, "odd")
        dg_codes = [per_pass([P, CLASSES], U32, "dg_codes_%d" % s) for s in range(TAPS)]
        dg_scales = [per_pass([P, CLASSES], U8, "dg_scales_%d" % s) for s in range(TAPS)]
        result = [keep.tile([P, M_TILES, CLASSES], F32, name="result_%d" % s) for s in range(TAPS)]
        edge_rows = per_pass([CHUNKS, PACK, CHUNK], BF16, "edge_rows")
        edge = per_pass([CHUNKS, CHUNK, PACK], BF16, "edge")

        one_down = keep.tile([P, 2 * P], BF16, name="one_down", align_bytes=64)

        a, b = 1, 0

        nc.gpsimd.memset(edge_rows[a][:], 0.0)
        nc.gpsimd.memset(one_down[:], 0.0)
        make_identity(nc, one_down[:, 0:P])

        def load(tiles, matrix, c, u):
            nc.sync.dma_start(out=tiles[c][:, u, :, :], in_=rows_of_pass(matrix, c)[:, u, :, :])

        def load_row(tiles, matrix, c, u, e):
            nc.sync.dma_start(out=tiles[c][:, u, e, :], in_=rows_of_pass(matrix, c)[:, u, e, :])

        def load_all(tiles, matrix, c):
            nc.sync.dma_start(out=tiles[c][:], in_=rows_of_pass(matrix, c))

        load(grad, grad_out, a, 1)
        load_row(prob, probs, a, 1, 0)
        load(grad, grad_out, a, 0)
        load_row(prob, probs, a, 1, 1)
        load(grad, grad_out, b, 1)
        load_row(prob, probs, a, 0, 0)
        load_row(prob, probs, a, 0, 1)
        load_row(prob, probs, b, 1, 0)
        load_all(hid, h, a)
        load(grad, grad_out, b, 0)
        load_row(prob, probs, b, 1, 1)
        load(prob, probs, b, 0)

        def minus_row_sums(c, u):
            for e in range(PAIR):
                t = PAIR * e + u
                nc.scalar.activation(
                    out=negated[c][:, t, :],
                    in_=grad[c][:, u, e, :],
                    func=mybir.ActivationFunctionType.Copy,
                    scale=-1.0,
                    accum_out=neg_sum[c][:, t : t + 1],
                )

        def make_dz_row(c, u, e):
            t = PAIR * e + u
            nc.vector.scalar_tensor_tensor(
                out=dz[c][:, t, :],
                in0=prob[c][:, u, e, :],
                scalar=neg_sum[c][:, t : t + 1],
                in1=grad[c][:, u, e, :],
                op0=mybir.AluOpType.mult,
                op1=mybir.AluOpType.add,
            )

        def make_dz(c, u):
            for e in range(PAIR):
                make_dz_row(c, u, e)

        def regroup_h(copy, c, cols):
            copy(
                out=h_grouped[c][:, cols, :].rearrange("p (c i) (e u) -> p c e u i", i=RUN, u=PAIR),
                in_=hid[c][:, :, :, cols].rearrange("p u e (c i) -> p c e u i", i=RUN),
            )

        def regroup_dz(copy, c, cols):
            copy(
                out=even[c][:, 0, cols, :].rearrange("p (c i) t -> p c t i", i=RUN),
                in_=dz[c][:, :, cols].rearrange("p t (c i) -> p c t i", i=RUN),
            )

        def flat(tile):
            return tile.rearrange("p w t -> p (w t)")

        def shift_by_two(c):
            for lo, hi in zip(SHIFT_CUTS, SHIFT_CUTS[1:]):
                nc.sync.dma_start(
                    out=flat(even[c][lo:hi, 1, :, :]), in_=flat(even[c][lo + 1 : hi + 1, 0, :, :])
                )

        def fetch_edge(c, u, c_from):
            for e in range(PAIR):
                t = PAIR * e + u
                row = dz[c_from][0:1, t + 1 - 2 * u, :]
                nc.sync.dma_start(out=edge_rows[c][:, t, :], in_=row.rearrange("o (q i) -> o q i", i=CHUNK))

        def place_edge(c):
            nc.gpsimd.tensor_copy(out=edge[c][:], in_=edge_rows[c][:].rearrange("q t i -> q i t"))
            nc.sync.dma_start(out=flat(even[c][P - 1 : P, 1, :, :]), in_=flat(edge[c][:]))

        def shift_by_one(copy, c):
            words = even[c][:].rearrange("p a w t -> p (a w t)").bitcast(F32)
            tile_words = CLASSES * PAIR
            pairs = words[:, 1 : 2 * tile_words - 1].rearrange("p (j x) -> p j x", j=PAIR)
            copy(
                out=flat(odd[c][:]).bitcast(F32).rearrange("p (c i j) -> p c j i", i=RUN, j=PAIR),
                in_=pairs[:, :, 0 : tile_words - 1 : PAIR].rearrange("p j (c i) -> p c j i", i=RUN),
            )

        def move_down(c, cols, bank):
            moved = psum.tile([P, HALF * PACK], BF16, tag="bank%d" % bank, name="moved_%d" % bank)
            for n in range(0, HALF * PACK, CLASSES):
                nc.tensor.matmul(
                    out=moved[:, n : n + CLASSES],
                    lhsT=one_down[:, 1 : 1 + P],
                    rhs=flat(even[c][:, 0, cols, :])[:, n : n + CLASSES],
                    start=True,
                    stop=True,
                )
            return moved

        def fetch_moved(copy, c, cols, moved):
            copy(out=flat(even[c][0 : P - 1, 1, cols, :]), in_=moved[0 : P - 1, :])

        def shifted(s, c):
            return flat(odd[c][:]) if s == 1 else flat(even[c][:, s // 2, :, :])

        def quantise_dg(s, c):
            nc.vector.quantize_mx(
                out=dg_codes[s][c][:].bitcast(E5M2_X4), scales=dg_scales[s][c][:], in_=shifted(s, c)
            )

        def quantise_h(c, cols):
            nc.vector.quantize_mx(
                out=h_codes[c][:, cols].bitcast(E4M3_X4),
                scales=h_scales[c][:, cols],
                in_=flat(h_grouped[c][:, cols, :]),
            )

        banks = {}

        def multiply(s, c, *ms):
            for m in ms:
                if c == a:
                    banks[s, m] = psum.tile(
                        [P, CLASSES], F32, tag="bank%d" % (M_TILES * (s // 2) + m), name="acc_%d_%d" % (s, m)
                    )
                m_cols = slice(m * P, (m + 1) * P)
                nc.tensor.matmul_mx(
                    out=banks[s, m][:],
                    lhsT=h_codes[c][:, m_cols].bitcast(E4M3_X4),
                    lhsT_scale=h_scales[c][:, m_cols],
                    rhs=dg_codes[s][c][:].bitcast(E5M2_X4),
                    rhs_scale=dg_scales[s][c][:],
                    start=(c == a),
                    stop=(c == b),
                )

        def store(copy, s, m):
            copy(out=result[s][:, m, :], in_=banks[s, m][:])
            nc.sync.dma_start(out=out[TAPS - 1 - s, m * P : (m + 1) * P, :], in_=result[s][:, m, :])

        on_vector, on_scalar = nc.vector.tensor_copy, nc.scalar.copy
        minus_row_sums(a, 1)
        minus_row_sums(a, 0)
        minus_row_sums(b, 1)
        make_dz(a, 1)
        make_dz(a, 0)
        fetch_edge(a, 0, a)
        fetch_edge(b, 1, a)
        load_all(hid, h, b)
        make_dz_row(b, 1, 0)
        regroup_dz(on_vector, a, LEFT)
        regroup_dz(on_scalar, a, RIGHT)
        shift_by_two(a)
        regroup_h(on_vector, a, LEFT)
        regroup_h(on_scalar, a, RIGHT)
        quantise_dg(0, a)
        minus_row_sums(b, 0)
        make_dz_row(b, 1, 1)
        quantise_h(a, LEFT)
        multiply(0, a, 0, 1)
        make_dz(b, 0)
        fetch_edge(b, 0, b)
        quantise_h(a, RIGHT)
        multiply(0, a, 2, 3)
        regroup_dz(on_vector, b, LEFT)
        regroup_dz(on_vector, b, RIGHT)
        moved_left = move_down(b, LEFT, 4)
        moved_right = move_down(b, RIGHT, 5)
        place_edge(a)
        regroup_h(on_scalar, b, LEFT)
        regroup_h(on_scalar, b, RIGHT)
        quantise_h(b, LEFT)
        quantise_dg(0, b)
        place_edge(b)
        multiply(0, b, 0, 1)
        quantise_h(b, RIGHT)
        multiply(0, b, 2, 3)
        fetch_moved(on_scalar, b, RIGHT, moved_right)
        for m in range(M_TILES):
            store(on_scalar, 0, m)
        quantise_dg(2, a)
        fetch_moved(on_vector, b, LEFT, moved_left)
        quantise_dg(2, b)
        multiply(2, a, 0, 1, 2)
        multiply(2, b, 0, 1)
        multiply(2, a, 3)
        multiply(2, b, 2, 3)
        for m in range(M_TILES):
            store(on_scalar, 2, m)
        shift_by_one(on_vector, a)
        shift_by_one(on_vector, b)
        quantise_dg(1, a)
        quantise_dg(1, b)
        for m in range(0, M_TILES, 2):
            multiply(1, a, m, m + 1)
            multiply(1, b, m, m + 1)
        for m in range(M_TILES):
            store((on_vector, on_scalar)[m % 2], 1, m)
